import numpy as np
import ml_dtypes

BF16 = ml_dtypes.bfloat16


def bf(x):
    return np.asarray(x, np.float32).astype(BF16)


def f32(x):
    return np.asarray(x, np.float32)


def f64(x):
    return np.asarray(x).astype(np.float64)


def striped(idx):
    return np.tile(idx.reshape(-1, 16).T, (8, 1))


C, S, N, A, NH, HD, H, K = 1024, 256, 1024, 4, 8, 128, 128, 8


def setup_inputs():
    x = f32(np.random.standard_normal((C, S)))
    wq = bf(np.random.standard_normal((C, C)) / np.sqrt(C))
    bq = f32(0.1 * np.random.standard_normal((C, 1)))
    idx = np.concatenate([np.random.permutation(S)[:H] for _ in range(K)])
    return {"x": x, "wq": wq, "bq": bq, "offs": striped(idx)}


def reference(x, wq, bq, offs):
    idx = offs[:16].T.reshape(-1)
    xs = f64(x)
    q = f64(wq).T @ xs + f64(bq)
    picked = xs[:, idx]
    prod = picked * np.repeat(q, A, axis=1)
    sim = prod.reshape(NH, HD, N).sum(axis=1) / np.sqrt(HD)
    e = np.exp(sim)
    den = e.reshape(NH, S, A).sum(axis=2)
    attn = e / np.repeat(den, A, axis=1)
    weighted = picked * np.repeat(attn, HD, axis=0)
    return weighted.reshape(C, S, A).sum(axis=2)

@@ -1,0 +1,112 @@
+from contextlib import ExitStack
+import math
+
+import concourse.mybir as mybir
+from concourse.masks import make_identity
+
+F32, BF16, U16 = mybir.dt.float32, mybir.dt.bfloat16, mybir.dt.uint16
+ALU = mybir.AluOpType
+ACT = mybir.ActivationFunctionType
+X_AXIS = mybir.AxisListType.X
+
+P = 128
+C, S, N, A = 1024, 256, 1024, 4
+HEADS = C // P
+PIECE = 256
+HALF = 512
+HALF_NODES = HALF // A
+SCALE = 1.0 / math.sqrt(P)
+
+FLOPS = 2 * C * C * S + 4 * C * N
+
+
+def tile_multiheaddotproduct_kernel(tc, x, wq, bq, offs, out):
+    nc = tc.nc
+    with ExitStack() as ctx:
+        held = ctx.enter_context(tc.tile_pool(name="held", bufs=1))
+        work = ctx.enter_context(tc.tile_pool(name="work", bufs=2))
+        psum = ctx.enter_context(tc.psum_pool(name="psum", bufs=2))
+
+        offsets = held.tile([P, N // 16], U16, name="offsets")
+        nc.sync.dma_start(offsets[:], offs)
+
+        ident = held.tile([P, P], F32, name="ident")
+        make_identity(nc, ident[:])
+        bq_rows = held.tile([P, P], F32, name="bq_rows")
+        nc.vector.memset(bq_rows[:], 0.0)
+        nc.sync.dma_start(bq_rows[0:HEADS, :], bq.rearrange("(h p) o -> h (p o)", p=P))
+        bq_ps = psum.tile([P, P], F32, name="bq_ps")
+        nc.tensor.transpose(bq_ps[:], bq_rows[:], ident[:])
+        bias = held.tile([P, HEADS], F32, name="bias")
+        nc.vector.tensor_copy(bias[:], bq_ps[:, 0:HEADS])
+
+        ones = held.tile([P, P], BF16, name="ones")
+        nc.vector.memset(ones[:], 1.0)
+
+        x_f32 = [held.tile([P, S], F32, name=f"x_f32_{h}") for h in range(HEADS)]
+        x_bf = [held.tile([P, S], BF16, name=f"x_bf_{h}") for h in range(HEADS)]
+        for h in range(HEADS):
+            nc.sync.dma_start(x_f32[h][:], x[h * P:(h + 1) * P, :])
+            nc.vector.tensor_copy(x_bf[h][:], x_f32[h][:])
+
+        wq_blocks = wq.rearrange("(ub p) c -> p ub c", p=P)
+        wq_sb = [held.tile([P, HEADS, P], BF16, name=f"wq_{h}") for h in range(HEADS)]
+        for h in range(HEADS):
+            nc.scalar.dma_start(wq_sb[h][:], wq_blocks[:, :, h * P:(h + 1) * P])
+
+        for h in range(HEADS):
+            q_ps = psum.tile([P, S], F32, name="q_ps")
+            for ub in range(HEADS):
+                nc.tensor.matmul(q_ps[:], lhsT=wq_sb[h][:, ub, :], rhs=x_bf[ub][:],
+                                 start=(ub == 0), stop=(ub == HEADS - 1))
+            q_rep = work.tile([P, N], F32, name="q_rep")
+            nc.scalar.activation(q_rep[:].rearrange("p (i a) -> p i a", a=A),
+                                 q_ps[:].unsqueeze(2).to_broadcast([P, S, A]),
+                                 ACT.Identity, bias=bias[:, h:h + 1])
+
+            o_sb = work.tile([P, S], F32, name="o_sb")
+            for half in range(N // HALF):
+                pieces = range(half * HALF // PIECE, (half + 1) * HALF // PIECE)
+
+                prod = work.tile([P, HALF], F32, name="prod")
+                for k, piece in enumerate(pieces):
+                    nc.vector.tensor_tensor(
+                        prod[:, k * PIECE:(k + 1) * PIECE],
+                        x_f32[h][:].indirect(offsets[:, piece * PIECE // 16:(piece + 1) * PIECE // 16]),
+                        q_rep[:, piece * PIECE:(piece + 1) * PIECE],
+                        ALU.mult)
+                prod_bf = work.tile([P, HALF], BF16, name="prod_bf")
+                nc.scalar.copy(prod_bf[:], prod[:])
+
+                sim_ps = psum.tile([P, HALF], F32, name="sim_ps")
+                nc.tensor.matmul(sim_ps[:], lhsT=ones[:], rhs=prod_bf[:], start=True, stop=True)
+                sim_by_node = sim_ps[:].rearrange("p (i a) -> p i a", a=A)
+
+                top = work.tile([P, HALF_NODES], F32, name="top")
+                nc.vector.tensor_reduce(top[:], sim_by_node, axis=X_AXIS, op=ALU.max)
+                shifted = work.tile([P, HALF], F32, name="shifted")
+                nc.vector.tensor_tensor(
+                    shifted[:].rearrange("p (i a) -> p i a", a=A), sim_by_node,
+                    top[:].unsqueeze(2).to_broadcast([P, HALF_NODES, A]), ALU.subtract)
+                e = work.tile([P, HALF], F32, name="e")
+                nc.scalar.activation(e[:], shifted[:], ACT.Exp, scale=SCALE)
+                den = work.tile([P, HALF_NODES], F32, name="den")
+                nc.vector.tensor_reduce(den[:], e[:].rearrange("p (i a) -> p i a", a=A),
+                                        axis=X_AXIS, op=ALU.add)
+                rden = work.tile([P, HALF_NODES], F32, name="rden")
+                nc.vector.reciprocal(rden[:], den[:])
+
+                weighted = work.tile([P, HALF], F32, name="weighted")
+                for k, piece in enumerate(pieces):
+                    nc.vector.tensor_tensor(
+                        weighted[:, k * PIECE:(k + 1) * PIECE],
+                        x_f32[h][:].indirect(offsets[:, piece * PIECE // 16:(piece + 1) * PIECE // 16]),
+                        e[:, k * PIECE:(k + 1) * PIECE],
+                        ALU.mult)
+                summed = work.tile([P, HALF_NODES], F32, name="summed")
+                nc.vector.tensor_reduce(summed[:], weighted[:].rearrange("p (i a) -> p i a", a=A),
+                                        axis=X_AXIS, op=ALU.add)
+                nc.vector.tensor_tensor(o_sb[:, half * HALF_NODES:(half + 1) * HALF_NODES],
+                                        summed[:], rden[:], ALU.mult)
+
+            nc.sync.dma_start(out[h * P:(h + 1) * P, :], o_sb[:])

@@ -13,8 +13,12 @@ P = 128
 C, S, N, A = 1024, 256, 1024, 4
 HEADS = C // P
 PIECE = 256
-HALF = 512
-HALF_NODES = HALF // A
+PIECES = N // PIECE
+STRIP = 64
+STRIP_NODES = STRIP // A
+ROWS_A_HEAD = N // STRIP
+GROUP = 2
+GROUP_ROWS = GROUP * ROWS_A_HEAD
 SCALE = 1.0 / math.sqrt(P)
 
 FLOPS = 2 * C * C * S + 4 * C * N
@@ -24,89 +28,116 @@ def tile_multiheaddotproduct_kernel(tc, x, wq, bq, offs, out):
     nc = tc.nc
     with ExitStack() as ctx:
         held = ctx.enter_context(tc.tile_pool(name="held", bufs=1))
-        work = ctx.enter_context(tc.tile_pool(name="work", bufs=2))
+        q_pool = ctx.enter_context(tc.tile_pool(name="q_pool", bufs=3))
+        prod_pool = ctx.enter_context(tc.tile_pool(name="prod_pool", bufs=8))
+        soft_pool = ctx.enter_context(tc.tile_pool(name="soft_pool", bufs=2))
+        out_pool = ctx.enter_context(tc.tile_pool(name="out_pool", bufs=4))
+        psum_once = ctx.enter_context(tc.psum_pool(name="psum_once", bufs=1))
         psum = ctx.enter_context(tc.psum_pool(name="psum", bufs=2))
 
         offsets = held.tile([P, N // 16], U16, name="offsets")
         nc.sync.dma_start(offsets[:], offs)
+
+        def piece_offsets(piece):
+            return offsets[:, piece * PIECE // 16:(piece + 1) * PIECE // 16]
 
         ident = held.tile([P, P], F32, name="ident")
         make_identity(nc, ident[:])
         bq_rows = held.tile([P, P], F32, name="bq_rows")
         nc.vector.memset(bq_rows[:], 0.0)
         nc.sync.dma_start(bq_rows[0:HEADS, :], bq.rearrange("(h p) o -> h (p o)", p=P))
-        bq_ps = psum.tile([P, P], F32, name="bq_ps")
+        bq_ps = psum_once.tile([P, P], F32, name="bq_ps")
         nc.tensor.transpose(bq_ps[:], bq_rows[:], ident[:])
         bias = held.tile([P, HEADS], F32, name="bias")
         nc.vector.tensor_copy(bias[:], bq_ps[:, 0:HEADS])
 
-        ones = held.tile([P, P], BF16, name="ones")
-        nc.vector.memset(ones[:], 1.0)
+        one_col = held.tile([P, 2 * P], BF16, name="one_col")
+        nc.vector.memset(one_col[:], 0.0)
+        nc.vector.memset(one_col[:, P - 1:P], 1.0)
 
         x_f32 = [held.tile([P, S], F32, name=f"x_f32_{h}") for h in range(HEADS)]
         x_bf = [held.tile([P, S], BF16, name=f"x_bf_{h}") for h in range(HEADS)]
+        wq_blocks = wq.rearrange("(ub p) c -> p ub c", p=P)
+        wq_sb = [held.tile([P, HEADS, P], BF16, name=f"wq_{h}") for h in range(HEADS)]
+        nc.sync.dma_start(wq_sb[0][:], wq_blocks[:, :, 0:P])
         for h in range(HEADS):
             nc.sync.dma_start(x_f32[h][:], x[h * P:(h + 1) * P, :])
             nc.vector.tensor_copy(x_bf[h][:], x_f32[h][:])
+        for h in range(1, HEADS):
+            nc.sync.dma_start(wq_sb[h][:], wq_blocks[:, :, h * P:(h + 1) * P])
 
-        wq_blocks = wq.rearrange("(ub p) c -> p ub c", p=P)
-        wq_sb = [held.tile([P, HEADS, P], BF16, name=f"wq_{h}") for h in range(HEADS)]
-        for h in range(HEADS):
-            nc.scalar.dma_start(wq_sb[h][:], wq_blocks[:, :, h * P:(h + 1) * P])
+        park_rows = HEADS * N // S
+        park = out[C - park_rows:C, :]
+        park_by_strip = park.rearrange("r (s t) -> (r s) t", t=STRIP)
+        attn_all = [held.tile([P, N], F32, name=f"attn_all_{h}") for h in range(HEADS)]
 
-        for h in range(HEADS):
+        def project(h):
             q_ps = psum.tile([P, S], F32, name="q_ps")
             for ub in range(HEADS):
                 nc.tensor.matmul(q_ps[:], lhsT=wq_sb[h][:, ub, :], rhs=x_bf[ub][:],
                                  start=(ub == 0), stop=(ub == HEADS - 1))
-            q_rep = work.tile([P, N], F32, name="q_rep")
+            q_rep = q_pool.tile([P, N], F32, name="q_rep")
             nc.scalar.activation(q_rep[:].rearrange("p (i a) -> p i a", a=A),
                                  q_ps[:].unsqueeze(2).to_broadcast([P, S, A]),
                                  ACT.Identity, bias=bias[:, h:h + 1])
+            return q_rep
 
-            o_sb = work.tile([P, S], F32, name="o_sb")
-            for half in range(N // HALF):
-                pieces = range(half * HALF // PIECE, (half + 1) * HALF // PIECE)
+        q_next = project(0)
+        for group in range(HEADS // GROUP):
+            first_row, end_row = group * GROUP_ROWS, (group + 1) * GROUP_ROWS
+            sims = psum.tile([P, STRIP], F32, name="sims")
+            for h in range(group * GROUP, (group + 1) * GROUP):
+                q_rep = q_next
+                if h + 1 < HEADS:
+                    q_next = project(h + 1)
 
-                prod = work.tile([P, HALF], F32, name="prod")
-                for k, piece in enumerate(pieces):
-                    nc.vector.tensor_tensor(
-                        prod[:, k * PIECE:(k + 1) * PIECE],
-                        x_f32[h][:].indirect(offsets[:, piece * PIECE // 16:(piece + 1) * PIECE // 16]),
-                        q_rep[:, piece * PIECE:(piece + 1) * PIECE],
-                        ALU.mult)
-                prod_bf = work.tile([P, HALF], BF16, name="prod_bf")
-                nc.scalar.copy(prod_bf[:], prod[:])
+                for piece in range(PIECES):
+                    prod = prod_pool.tile([P, PIECE], F32, name="prod")
+                    nc.vector.tensor_tensor(prod[:], x_f32[h][:].indirect(piece_offsets(piece)),
+                                            q_rep[:, piece * PIECE:(piece + 1) * PIECE], ALU.mult)
+                    prod_bf = prod_pool.tile([P, PIECE], BF16, name="prod_bf")
+                    nc.scalar.copy(prod_bf[:], prod[:])
+                    for s in range(PIECE // STRIP):
+                        row = h * ROWS_A_HEAD + piece * (PIECE // STRIP) + s
+                        nc.tensor.matmul(sims[:], lhsT=one_col[:, P - 1 - row:2 * P - 1 - row],
+                                         rhs=prod_bf[:, s * STRIP:(s + 1) * STRIP],
+                                         start=(row == first_row), stop=(row == end_row - 1))
 
-                sim_ps = psum.tile([P, HALF], F32, name="sim_ps")
-                nc.tensor.matmul(sim_ps[:], lhsT=ones[:], rhs=prod_bf[:], start=True, stop=True)
-                sim_by_node = sim_ps[:].rearrange("p (i a) -> p i a", a=A)
+            sims_by_node = sims[:].rearrange("p (i a) -> p i a", a=A)
+            top = soft_pool.tile([P, STRIP_NODES], F32, name="top")
+            nc.vector.tensor_reduce(top[:], sims_by_node, axis=X_AXIS, op=ALU.max)
+            shifted = soft_pool.tile([P, STRIP], F32, name="shifted")
+            nc.vector.tensor_tensor(shifted[:].rearrange("p (i a) -> p i a", a=A), sims_by_node,
+                                    top[:].unsqueeze(2).to_broadcast([P, STRIP_NODES, A]),
+                                    ALU.subtract)
+            e = soft_pool.tile([P, STRIP], F32, name="e")
+            nc.scalar.activation(e[:], shifted[:], ACT.Exp, scale=SCALE)
+            e_by_node = e[:].rearrange("p (i a) -> p i a", a=A)
+            den = soft_pool.tile([P, STRIP_NODES], F32, name="den")
+            nc.vector.tensor_reduce(den[:], e_by_node, axis=X_AXIS, op=ALU.add)
+            rden = soft_pool.tile([P, STRIP_NODES], F32, name="rden")
+            nc.vector.reciprocal(rden[:], den[:])
+            attn = soft_pool.tile([P, STRIP], F32, name="attn")
+            nc.vector.tensor_tensor(attn[:].rearrange("p (i a) -> p i a", a=A), e_by_node,
+                                    rden[:].unsqueeze(2).to_broadcast([P, STRIP_NODES, A]),
+                                    ALU.mult)
 
-                top = work.tile([P, HALF_NODES], F32, name="top")
-                nc.vector.tensor_reduce(top[:], sim_by_node, axis=X_AXIS, op=ALU.max)
-                shifted = work.tile([P, HALF], F32, name="shifted")
-                nc.vector.tensor_tensor(
-                    shifted[:].rearrange("p (i a) -> p i a", a=A), sim_by_node,
-                    top[:].unsqueeze(2).to_broadcast([P, HALF_NODES, A]), ALU.subtract)
-                e = work.tile([P, HALF], F32, name="e")
-                nc.scalar.activation(e[:], shifted[:], ACT.Exp, scale=SCALE)
-                den = work.tile([P, HALF_NODES], F32, name="den")
-                nc.vector.tensor_reduce(den[:], e[:].rearrange("p (i a) -> p i a", a=A),
-                                        axis=X_AXIS, op=ALU.add)
-                rden = work.tile([P, HALF_NODES], F32, name="rden")
-                nc.vector.reciprocal(rden[:], den[:])
+            nc.sync.dma_start(park_by_strip[first_row:end_row, :], attn[first_row:end_row, :])
+            for h in range(group * GROUP, (group + 1) * GROUP):
+                head_park = park[h * N // S:(h + 1) * N // S, :].rearrange("r c -> (r c)")
+                nc.sync.dma_start(attn_all[h][:], head_park.partition_broadcast(P))
 
-                weighted = work.tile([P, HALF], F32, name="weighted")
-                for k, piece in enumerate(pieces):
-                    nc.vector.tensor_tensor(
-                        weighted[:, k * PIECE:(k + 1) * PIECE],
-                        x_f32[h][:].indirect(offsets[:, piece * PIECE // 16:(piece + 1) * PIECE // 16]),
-                        e[:, k * PIECE:(k + 1) * PIECE],
-                        ALU.mult)
-                summed = work.tile([P, HALF_NODES], F32, name="summed")
-                nc.vector.tensor_reduce(summed[:], weighted[:].rearrange("p (i a) -> p i a", a=A),
-                                        axis=X_AXIS, op=ALU.add)
-                nc.vector.tensor_tensor(o_sb[:, half * HALF_NODES:(half + 1) * HALF_NODES],
-                                        summed[:], rden[:], ALU.mult)
-
+        for h in range(HEADS):
+            weighted = out_pool.tile([P, N], F32, name="weighted")
+            for piece in range(PIECES):
+                cols = slice(piece * PIECE, (piece + 1) * PIECE)
+                nc.vector.tensor_tensor(weighted[:, cols], x_f32[h][:].indirect(piece_offsets(piece)),
+                                        attn_all[h][:, cols], ALU.mult)
+            weighted_by_node = weighted[:].rearrange("p (i a) -> p i a", a=A)
+            o_ps = psum.tile([P, S], F32, name="o_ps")
+            for a in range(A):
+                nc.tensor.matmul(o_ps[:], lhsT=ident[:], rhs=weighted_by_node[:, :, a],
+                                 start=(a == 0), stop=(a == A - 1))
+            o_sb = out_pool.tile([P, S], F32, name="o_sb")
+            nc.scalar.copy(o_sb[:], o_ps[:])
             nc.sync.dma_start(out[h * P:(h + 1) * P, :], o_sb[:])

@@ -128,15 +128,16 @@ def tile_multiheaddotproduct_kernel(tc, x, wq, bq, offs, out):
                 nc.sync.dma_start(attn_all[h][:], head_park.partition_broadcast(P))
 
         for h in range(HEADS):
-            weighted = out_pool.tile([P, N], F32, name="weighted")
+            planes = out_pool.tile([P, A, S], F32, name="planes")
             for piece in range(PIECES):
-                cols = slice(piece * PIECE, (piece + 1) * PIECE)
-                nc.vector.tensor_tensor(weighted[:, cols], x_f32[h][:].indirect(piece_offsets(piece)),
-                                        attn_all[h][:, cols], ALU.mult)
-            weighted_by_node = weighted[:].rearrange("p (i a) -> p i a", a=A)
+                weighted = prod_pool.tile([P, PIECE], F32, name="weighted")
+                nc.vector.tensor_tensor(weighted[:], x_f32[h][:].indirect(piece_offsets(piece)),
+                                        attn_all[h][:, piece * PIECE:(piece + 1) * PIECE], ALU.mult)
+                nc.scalar.copy(planes[:, :, piece * PIECE // A:(piece + 1) * PIECE // A],
+                               weighted[:].rearrange("p (i a) -> p a i", a=A))
             o_ps = psum.tile([P, S], F32, name="o_ps")
             for a in range(A):
-                nc.tensor.matmul(o_ps[:], lhsT=ident[:], rhs=weighted_by_node[:, :, a],
+                nc.tensor.matmul(o_ps[:], lhsT=ident[:], rhs=planes[:, a, :],
                                  start=(a == 0), stop=(a == A - 1))
             o_sb = out_pool.tile([P, S], F32, name="o_sb")
             nc.scalar.copy(o_sb[:], o_ps[:])

@@ -133,8 +133,9 @@ def tile_multiheaddotproduct_kernel(tc, x, wq, bq, offs, out):
                 weighted = prod_pool.tile([P, PIECE], F32, name="weighted")
                 nc.vector.tensor_tensor(weighted[:], x_f32[h][:].indirect(piece_offsets(piece)),
                                         attn_all[h][:, piece * PIECE:(piece + 1) * PIECE], ALU.mult)
-                nc.scalar.copy(planes[:, :, piece * PIECE // A:(piece + 1) * PIECE // A],
-                               weighted[:].rearrange("p (i a) -> p a i", a=A))
+                nc.scalar.copy(planes[:, :, piece * PIECE // A:(piece + 1) * PIECE // A]
+                               .rearrange("p a i -> p i a"),
+                               weighted[:].rearrange("p (i a) -> p i a", a=A))
             o_ps = psum.tile([P, S], F32, name="o_ps")
             for a in range(A):
                 nc.tensor.matmul(o_ps[:], lhsT=ident[:], rhs=planes[:, a, :],

@@ -28,8 +28,8 @@ def tile_multiheaddotproduct_kernel(tc, x, wq, bq, offs, out):
     nc = tc.nc
     with ExitStack() as ctx:
         held = ctx.enter_context(tc.tile_pool(name="held", bufs=1))
-        q_pool = ctx.enter_context(tc.tile_pool(name="q_pool", bufs=3))
-        prod_pool = ctx.enter_context(tc.tile_pool(name="prod_pool", bufs=8))
+        prod_pool = ctx.enter_context(tc.tile_pool(name="prod_pool", bufs=HEADS * PIECES))
+        weighted_pool = ctx.enter_context(tc.tile_pool(name="weighted_pool", bufs=8))
         soft_pool = ctx.enter_context(tc.tile_pool(name="soft_pool", bufs=2))
         out_pool = ctx.enter_context(tc.tile_pool(name="out_pool", bufs=4))
         psum_once = ctx.enter_context(tc.psum_pool(name="psum_once", bufs=1))
@@ -71,30 +71,24 @@ def tile_multiheaddotproduct_kernel(tc, x, wq, bq, offs, out):
         park_by_strip = park.rearrange("r (s t) -> (r s) t", t=STRIP)
         attn_all = [held.tile([P, N], F32, name=f"attn_all_{h}") for h in range(HEADS)]
 
-        def project(h):
+        q_rep = [held.tile([P, N], F32, name=f"q_rep_{h}") for h in range(HEADS)]
+        for h in range(HEADS):
             q_ps = psum.tile([P, S], F32, name="q_ps")
             for ub in range(HEADS):
                 nc.tensor.matmul(q_ps[:], lhsT=wq_sb[h][:, ub, :], rhs=x_bf[ub][:],
                                  start=(ub == 0), stop=(ub == HEADS - 1))
-            q_rep = q_pool.tile([P, N], F32, name="q_rep")
-            nc.scalar.activation(q_rep[:].rearrange("p (i a) -> p i a", a=A),
+            nc.scalar.activation(q_rep[h][:].rearrange("p (i a) -> p i a", a=A),
                                  q_ps[:].unsqueeze(2).to_broadcast([P, S, A]),
                                  ACT.Identity, bias=bias[:, h:h + 1])
-            return q_rep
 
-        q_next = project(0)
         for group in range(HEADS // GROUP):
             first_row, end_row = group * GROUP_ROWS, (group + 1) * GROUP_ROWS
             sims = psum.tile([P, STRIP], F32, name="sims")
             for h in range(group * GROUP, (group + 1) * GROUP):
-                q_rep = q_next
-                if h + 1 < HEADS:
-                    q_next = project(h + 1)
-
                 for piece in range(PIECES):
                     prod = prod_pool.tile([P, PIECE], F32, name="prod")
                     nc.vector.tensor_tensor(prod[:], x_f32[h][:].indirect(piece_offsets(piece)),
-                                            q_rep[:, piece * PIECE:(piece + 1) * PIECE], ALU.mult)
+                                            q_rep[h][:, piece * PIECE:(piece + 1) * PIECE], ALU.mult)
                     prod_bf = prod_pool.tile([P, PIECE], BF16, name="prod_bf")
                     nc.scalar.copy(prod_bf[:], prod[:])
                     for s in range(PIECE // STRIP):
@@ -130,7 +124,7 @@ def tile_multiheaddotproduct_kernel(tc, x, wq, bq, offs, out):
         for h in range(HEADS):
             planes = out_pool.tile([P, A, S], F32, name="planes")
             for piece in range(PIECES):
-                weighted = prod_pool.tile([P, PIECE], F32, name="weighted")
+                weighted = weighted_pool.tile([P, PIECE], F32, name="weighted")
                 nc.vector.tensor_tensor(weighted[:], x_f32[h][:].indirect(piece_offsets(piece)),
                                         attn_all[h][:, piece * PIECE:(piece + 1) * PIECE], ALU.mult)
                 nc.scalar.copy(planes[:, :, piece * PIECE // A:(piece + 1) * PIECE // A]

@@ -28,8 +28,8 @@ def tile_multiheaddotproduct_kernel(tc, x, wq, bq, offs, out):
     nc = tc.nc
     with ExitStack() as ctx:
         held = ctx.enter_context(tc.tile_pool(name="held", bufs=1))
-        prod_pool = ctx.enter_context(tc.tile_pool(name="prod_pool", bufs=HEADS * PIECES))
-        weighted_pool = ctx.enter_context(tc.tile_pool(name="weighted_pool", bufs=8))
+        q_pool = ctx.enter_context(tc.tile_pool(name="q_pool", bufs=3))
+        prod_pool = ctx.enter_context(tc.tile_pool(name="prod_pool", bufs=8))
         soft_pool = ctx.enter_context(tc.tile_pool(name="soft_pool", bufs=2))
         out_pool = ctx.enter_context(tc.tile_pool(name="out_pool", bufs=4))
         psum_once = ctx.enter_context(tc.psum_pool(name="psum_once", bufs=1))
@@ -71,24 +71,30 @@ def tile_multiheaddotproduct_kernel(tc, x, wq, bq, offs, out):
         park_by_strip = park.rearrange("r (s t) -> (r s) t", t=STRIP)
         attn_all = [held.tile([P, N], F32, name=f"attn_all_{h}") for h in range(HEADS)]
 
-        q_rep = [held.tile([P, N], F32, name=f"q_rep_{h}") for h in range(HEADS)]
-        for h in range(HEADS):
+        def project(h):
             q_ps = psum.tile([P, S], F32, name="q_ps")
             for ub in range(HEADS):
                 nc.tensor.matmul(q_ps[:], lhsT=wq_sb[h][:, ub, :], rhs=x_bf[ub][:],
                                  start=(ub == 0), stop=(ub == HEADS - 1))
-            nc.scalar.activation(q_rep[h][:].rearrange("p (i a) -> p i a", a=A),
+            q_rep = q_pool.tile([P, N], F32, name="q_rep")
+            nc.scalar.activation(q_rep[:].rearrange("p (i a) -> p i a", a=A),
                                  q_ps[:].unsqueeze(2).to_broadcast([P, S, A]),
                                  ACT.Identity, bias=bias[:, h:h + 1])
+            return q_rep
 
+        q_next = project(0)
         for group in range(HEADS // GROUP):
             first_row, end_row = group * GROUP_ROWS, (group + 1) * GROUP_ROWS
             sims = psum.tile([P, STRIP], F32, name="sims")
             for h in range(group * GROUP, (group + 1) * GROUP):
+                q_rep = q_next
+                if h + 1 < HEADS:
+                    q_next = project(h + 1)
+
                 for piece in range(PIECES):
                     prod = prod_pool.tile([P, PIECE], F32, name="prod")
                     nc.vector.tensor_tensor(prod[:], x_f32[h][:].indirect(piece_offsets(piece)),
-                                            q_rep[h][:, piece * PIECE:(piece + 1) * PIECE], ALU.mult)
+                                            q_rep[:, piece * PIECE:(piece + 1) * PIECE], ALU.mult)
                     prod_bf = prod_pool.tile([P, PIECE], BF16, name="prod_bf")
                     nc.scalar.copy(prod_bf[:], prod[:])
                     for s in range(PIECE // STRIP):
@@ -122,18 +128,26 @@ def tile_multiheaddotproduct_kernel(tc, x, wq, bq, offs, out):
                 nc.sync.dma_start(attn_all[h][:], head_park.partition_broadcast(P))
 
         for h in range(HEADS):
-            planes = out_pool.tile([P, A, S], F32, name="planes")
+            on_tensor = h % 2 == 0
+            weighted = out_pool.tile([P, N], F32, name="weighted")
+            if on_tensor:
+                planes = out_pool.tile([P, A, S], F32, name="planes")
             for piece in range(PIECES):
-                weighted = weighted_pool.tile([P, PIECE], F32, name="weighted")
-                nc.vector.tensor_tensor(weighted[:], x_f32[h][:].indirect(piece_offsets(piece)),
+                weighted_piece = weighted[:, piece * PIECE:(piece + 1) * PIECE]
+                nc.vector.tensor_tensor(weighted_piece, x_f32[h][:].indirect(piece_offsets(piece)),
                                         attn_all[h][:, piece * PIECE:(piece + 1) * PIECE], ALU.mult)
-                nc.scalar.copy(planes[:, :, piece * PIECE // A:(piece + 1) * PIECE // A]
-                               .rearrange("p a i -> p i a"),
-                               weighted[:].rearrange("p (i a) -> p i a", a=A))
-            o_ps = psum.tile([P, S], F32, name="o_ps")
-            for a in range(A):
-                nc.tensor.matmul(o_ps[:], lhsT=ident[:], rhs=planes[:, a, :],
-                                 start=(a == 0), stop=(a == A - 1))
+                if on_tensor:
+                    nc.scalar.copy(planes[:, :, piece * PIECE // A:(piece + 1) * PIECE // A]
+                                   .rearrange("p a i -> p i a"),
+                                   weighted_piece.rearrange("p (i a) -> p i a", a=A))
             o_sb = out_pool.tile([P, S], F32, name="o_sb")
-            nc.scalar.copy(o_sb[:], o_ps[:])
+            if on_tensor:
+                o_ps = psum.tile([P, S], F32, name="o_ps")
+                for a in range(A):
+                    nc.tensor.matmul(o_ps[:], lhsT=ident[:], rhs=planes[:, a, :],
+                                     start=(a == 0), stop=(a == A - 1))
+                nc.scalar.copy(o_sb[:], o_ps[:])
+            else:
+                nc.vector.tensor_reduce(o_sb[:], weighted[:].rearrange("p (i a) -> p i a", a=A),
+                                        axis=X_AXIS, op=ALU.add)
             nc.sync.dma_start(out[h * P:(h + 1) * P, :], o_sb[:])

@@ -14,11 +14,11 @@ C, S, N, A = 1024, 256, 1024, 4
 HEADS = C // P
 PIECE = 256
 PIECES = N // PIECE
+PIECE_NODES = PIECE // A
 STRIP = 64
 STRIP_NODES = STRIP // A
 ROWS_A_HEAD = N // STRIP
-GROUP = 2
-GROUP_ROWS = GROUP * ROWS_A_HEAD
+GROUP = 3
 SCALE = 1.0 / math.sqrt(P)
 
 FLOPS = 2 * C * C * S + 4 * C * N
@@ -51,9 +51,14 @@ def tile_multiheaddotproduct_kernel(tc, x, wq, bq, offs, out):
         bias = held.tile([P, HEADS], F32, name="bias")
         nc.vector.tensor_copy(bias[:], bq_ps[:, 0:HEADS])
 
-        one_col = held.tile([P, 2 * P], BF16, name="one_col")
-        nc.vector.memset(one_col[:], 0.0)
-        nc.vector.memset(one_col[:, P - 1:P], 1.0)
+        one_col = [held.tile([P, 2 * P], BF16, name=f"one_col_{odd}") for odd in range(2)]
+        for odd in range(2):
+            nc.vector.memset(one_col[odd][:], 0.0)
+            nc.vector.memset(one_col[odd][:, P - odd:P - odd + 1], 1.0)
+
+        def sum_into_row(row):
+            first_col = P - row % 2 - row
+            return one_col[row % 2][:, first_col:first_col + P]
 
         x_f32 = [held.tile([P, S], F32, name=f"x_f32_{h}") for h in range(HEADS)]
         x_bf = [held.tile([P, S], BF16, name=f"x_bf_{h}") for h in range(HEADS)]
@@ -77,16 +82,20 @@ def tile_multiheaddotproduct_kernel(tc, x, wq, bq, offs, out):
                 nc.tensor.matmul(q_ps[:], lhsT=wq_sb[h][:, ub, :], rhs=x_bf[ub][:],
                                  start=(ub == 0), stop=(ub == HEADS - 1))
             q_rep = q_pool.tile([P, N], F32, name="q_rep")
-            nc.scalar.activation(q_rep[:].rearrange("p (i a) -> p i a", a=A),
-                                 q_ps[:].unsqueeze(2).to_broadcast([P, S, A]),
-                                 ACT.Identity, bias=bias[:, h:h + 1])
+            for piece in range(PIECES):
+                nc.scalar.activation(
+                    q_rep[:, piece * PIECE:(piece + 1) * PIECE].rearrange("p (i a) -> p i a", a=A),
+                    q_ps[:, piece * PIECE_NODES:(piece + 1) * PIECE_NODES]
+                    .unsqueeze(2).to_broadcast([P, PIECE_NODES, A]),
+                    ACT.Identity, bias=bias[:, h:h + 1])
             return q_rep
 
         q_next = project(0)
-        for group in range(HEADS // GROUP):
-            first_row, end_row = group * GROUP_ROWS, (group + 1) * GROUP_ROWS
+        for first_head in range(0, HEADS, GROUP):
+            end_head = min(first_head + GROUP, HEADS)
+            first_row, end_row = first_head * ROWS_A_HEAD, end_head * ROWS_A_HEAD
             sims = psum.tile([P, STRIP], F32, name="sims")
-            for h in range(group * GROUP, (group + 1) * GROUP):
+            for h in range(first_head, end_head):
                 q_rep = q_next
                 if h + 1 < HEADS:
                     q_next = project(h + 1)
@@ -99,7 +108,7 @@ def tile_multiheaddotproduct_kernel(tc, x, wq, bq, offs, out):
                     nc.scalar.copy(prod_bf[:], prod[:])
                     for s in range(PIECE // STRIP):
                         row = h * ROWS_A_HEAD + piece * (PIECE // STRIP) + s
-                        nc.tensor.matmul(sims[:], lhsT=one_col[:, P - 1 - row:2 * P - 1 - row],
+                        nc.tensor.matmul(sims[:], lhsT=sum_into_row(row),
                                          rhs=prod_bf[:, s * STRIP:(s + 1) * STRIP],
                                          start=(row == first_row), stop=(row == end_row - 1))
 
@@ -123,12 +132,12 @@ def tile_multiheaddotproduct_kernel(tc, x, wq, bq, offs, out):
                                     ALU.mult)
 
             nc.sync.dma_start(park_by_strip[first_row:end_row, :], attn[first_row:end_row, :])
-            for h in range(group * GROUP, (group + 1) * GROUP):
+            for h in range(first_head, end_head):
                 head_park = park[h * N // S:(h + 1) * N // S, :].rearrange("r c -> (r c)")
                 nc.sync.dma_start(attn_all[h][:], head_park.partition_broadcast(P))
 
         for h in range(HEADS):
-            on_tensor = h % 2 == 0
+            on_tensor = (h + 1) % GROUP != 0 and h != HEADS - 1
             weighted = out_pool.tile([P, N], F32, name="weighted")
             if on_tensor:
                 planes = out_pool.tile([P, A, S], F32, name="planes")
@@ -137,15 +146,17 @@ def tile_multiheaddotproduct_kernel(tc, x, wq, bq, offs, out):
                 nc.vector.tensor_tensor(weighted_piece, x_f32[h][:].indirect(piece_offsets(piece)),
                                         attn_all[h][:, piece * PIECE:(piece + 1) * PIECE], ALU.mult)
                 if on_tensor:
-                    nc.scalar.copy(planes[:, :, piece * PIECE // A:(piece + 1) * PIECE // A]
+                    nc.scalar.copy(planes[:, :, piece * PIECE_NODES:(piece + 1) * PIECE_NODES]
                                    .rearrange("p a i -> p i a"),
                                    weighted_piece.rearrange("p (i a) -> p i a", a=A))
             o_sb = out_pool.tile([P, S], F32, name="o_sb")
             if on_tensor:
                 o_ps = psum.tile([P, S], F32, name="o_ps")
-                for a in range(A):
-                    nc.tensor.matmul(o_ps[:], lhsT=ident[:], rhs=planes[:, a, :],
-                                     start=(a == 0), stop=(a == A - 1))
+                for half in range(2):
+                    for a in range(A):
+                        nc.tensor.matmul(o_ps[:, half * S // 2:(half + 1) * S // 2], lhsT=ident[:],
+                                         rhs=planes[:, a, half * S // 2:(half + 1) * S // 2],
+                                         start=(a == 0), stop=(a == A - 1))
                 nc.scalar.copy(o_sb[:], o_ps[:])
             else:
                 nc.vector.tensor_reduce(o_sb[:], weighted[:].rearrange("p (i a) -> p i a", a=A),

@@ -29,7 +29,7 @@ def tile_multiheaddotproduct_kernel(tc, x, wq, bq, offs, out):
     with ExitStack() as ctx:
         held = ctx.enter_context(tc.tile_pool(name="held", bufs=1))
         q_pool = ctx.enter_context(tc.tile_pool(name="q_pool", bufs=3))
-        prod_pool = ctx.enter_context(tc.tile_pool(name="prod_pool", bufs=8))
+        prod_pool = ctx.enter_context(tc.tile_pool(name="prod_pool", bufs=4))
         soft_pool = ctx.enter_context(tc.tile_pool(name="soft_pool", bufs=2))
         out_pool = ctx.enter_context(tc.tile_pool(name="out_pool", bufs=4))
         psum_once = ctx.enter_context(tc.psum_pool(name="psum_once", bufs=1))
@@ -82,11 +82,12 @@ def tile_multiheaddotproduct_kernel(tc, x, wq, bq, offs, out):
                 nc.tensor.matmul(q_ps[:], lhsT=wq_sb[h][:, ub, :], rhs=x_bf[ub][:],
                                  start=(ub == 0), stop=(ub == HEADS - 1))
             q_rep = q_pool.tile([P, N], F32, name="q_rep")
-            for piece in range(PIECES):
+            cuts = PIECES if h == 0 else 1
+            for cut in range(cuts):
                 nc.scalar.activation(
-                    q_rep[:, piece * PIECE:(piece + 1) * PIECE].rearrange("p (i a) -> p i a", a=A),
-                    q_ps[:, piece * PIECE_NODES:(piece + 1) * PIECE_NODES]
-                    .unsqueeze(2).to_broadcast([P, PIECE_NODES, A]),
+                    q_rep[:, cut * N // cuts:(cut + 1) * N // cuts].rearrange("p (i a) -> p i a", a=A),
+                    q_ps[:, cut * S // cuts:(cut + 1) * S // cuts]
+                    .unsqueeze(2).to_broadcast([P, S // cuts, A]),
                     ACT.Identity, bias=bias[:, h:h + 1])
             return q_rep
 
@@ -100,14 +101,16 @@ def tile_multiheaddotproduct_kernel(tc, x, wq, bq, offs, out):
                 if h + 1 < HEADS:
                     q_next = project(h + 1)
 
-                for piece in range(PIECES):
-                    prod = prod_pool.tile([P, PIECE], F32, name="prod")
-                    nc.vector.tensor_tensor(prod[:], x_f32[h][:].indirect(piece_offsets(piece)),
-                                            q_rep[:, piece * PIECE:(piece + 1) * PIECE], ALU.mult)
-                    prod_bf = prod_pool.tile([P, PIECE], BF16, name="prod_bf")
+                for pair in range(PIECES // 2):
+                    prod = prod_pool.tile([P, 2 * PIECE], F32, name="prod")
+                    for piece in (2 * pair, 2 * pair + 1):
+                        nc.vector.tensor_tensor(prod[:, (piece % 2) * PIECE:(piece % 2 + 1) * PIECE],
+                                                x_f32[h][:].indirect(piece_offsets(piece)),
+                                                q_rep[:, piece * PIECE:(piece + 1) * PIECE], ALU.mult)
+                    prod_bf = prod_pool.tile([P, 2 * PIECE], BF16, name="prod_bf")
                     nc.scalar.copy(prod_bf[:], prod[:])
-                    for s in range(PIECE // STRIP):
-                        row = h * ROWS_A_HEAD + piece * (PIECE // STRIP) + s
+                    for s in range(2 * PIECE // STRIP):
+                        row = h * ROWS_A_HEAD + pair * (2 * PIECE // STRIP) + s
                         nc.tensor.matmul(sims[:], lhsT=sum_into_row(row),
                                          rhs=prod_bf[:, s * STRIP:(s + 1) * STRIP],
                                          start=(row == first_row), stop=(row == end_row - 1))

@@ -19,6 +19,7 @@ STRIP = 64
 STRIP_NODES = STRIP // A
 ROWS_A_HEAD = N // STRIP
 GROUP = 3
+STORE_ROWS = 64
 SCALE = 1.0 / math.sqrt(P)
 
 FLOPS = 2 * C * C * S + 4 * C * N
@@ -134,7 +135,8 @@ def tile_multiheaddotproduct_kernel(tc, x, wq, bq, offs, out):
                                     rden[:].unsqueeze(2).to_broadcast([P, STRIP_NODES, A]),
                                     ALU.mult)
 
-            nc.sync.dma_start(park_by_strip[first_row:end_row, :], attn[first_row:end_row, :])
+            store_end = min(first_row + STORE_ROWS, P)
+            nc.sync.dma_start(park_by_strip[first_row:store_end, :], attn[first_row:store_end, :])
             for h in range(first_head, end_head):
                 head_park = park[h * N // S:(h + 1) * N // S, :].rearrange("r c -> (r c)")
                 nc.sync.dma_start(attn_all[h][:], head_park.partition_broadcast(P))

@@ -104,12 +104,16 @@ def tile_multiheaddotproduct_kernel(tc, x, wq, bq, offs, out):
 
                 for pair in range(PIECES // 2):
                     prod = prod_pool.tile([P, 2 * PIECE], F32, name="prod")
-                    for piece in (2 * pair, 2 * pair + 1):
-                        nc.vector.tensor_tensor(prod[:, (piece % 2) * PIECE:(piece % 2 + 1) * PIECE],
-                                                x_f32[h][:].indirect(piece_offsets(piece)),
-                                                q_rep[:, piece * PIECE:(piece + 1) * PIECE], ALU.mult)
                     prod_bf = prod_pool.tile([P, 2 * PIECE], BF16, name="prod_bf")
-                    nc.scalar.copy(prod_bf[:], prod[:])
+                    last_of_group = h == end_head - 1 and pair == PIECES // 2 - 1
+                    for piece in (2 * pair, 2 * pair + 1):
+                        cols = slice((piece % 2) * PIECE, (piece % 2 + 1) * PIECE)
+                        nc.vector.tensor_tensor(prod[:, cols], x_f32[h][:].indirect(piece_offsets(piece)),
+                                                q_rep[:, piece * PIECE:(piece + 1) * PIECE], ALU.mult)
+                        if last_of_group:
+                            nc.scalar.copy(prod_bf[:, cols], prod[:, cols])
+                    if not last_of_group:
+                        nc.scalar.copy(prod_bf[:], prod[:])
                     for s in range(2 * PIECE // STRIP):
                         row = h * ROWS_A_HEAD + pair * (2 * PIECE // STRIP) + s
                         nc.tensor.matmul(sims[:], lhsT=sum_into_row(row),
@@ -142,7 +146,7 @@ def tile_multiheaddotproduct_kernel(tc, x, wq, bq, offs, out):
                 nc.sync.dma_start(attn_all[h][:], head_park.partition_broadcast(P))
 
         for h in range(HEADS):
-            on_tensor = (h + 1) % GROUP != 0 and h != HEADS - 1
+            on_tensor = h not in (2 * GROUP - 1, HEADS - 1)
             weighted = out_pool.tile([P, N], F32, name="weighted")
             if on_tensor:
                 planes = out_pool.tile([P, A, S], F32, name="planes")
@@ -163,7 +167,8 @@ def tile_multiheaddotproduct_kernel(tc, x, wq, bq, offs, out):
                                          rhs=planes[:, a, half * S // 2:(half + 1) * S // 2],
                                          start=(a == 0), stop=(a == A - 1))
                 nc.scalar.copy(o_sb[:], o_ps[:])
+                nc.scalar.dma_start(out[h * P:(h + 1) * P, :], o_sb[:])
             else:
                 nc.vector.tensor_reduce(o_sb[:], weighted[:].rearrange("p (i a) -> p i a", a=A),
                                         axis=X_AXIS, op=ALU.add)
-            nc.sync.dma_start(out[h * P:(h + 1) * P, :], o_sb[:])
+                nc.sync.dma_start(out[h * P:(h + 1) * P, :], o_sb[:])

@@ -19,6 +19,7 @@ STRIP = 64
 STRIP_NODES = STRIP // A
 ROWS_A_HEAD = N // STRIP
 GROUP = 3
+CHUNKS = ((1, 3), (3, 5), (5, 7), (7, 8))
 STORE_ROWS = 64
 SCALE = 1.0 / math.sqrt(P)
 
@@ -36,21 +37,35 @@ def tile_multiheaddotproduct_kernel(tc, x, wq, bq, offs, out):
         psum_once = ctx.enter_context(tc.psum_pool(name="psum_once", bufs=1))
         psum = ctx.enter_context(tc.psum_pool(name="psum", bufs=2))
 
+        x_blocks = x.rearrange("(ub p) s -> p ub s", p=P)
+        wq_blocks = wq.rearrange("(ub p) c -> p ub c", p=P)
+        wq_sb = [held.tile([P, HEADS, P], BF16, name=f"wq_{h}") for h in range(HEADS)]
+        x_f32 = [held.tile([P, S], F32, name=f"x_f32_{h}") for h in range(HEADS)]
+        x_chunks = [held.tile([P, end - first, S], F32, name=f"x_chunk_{first}") for first, end in CHUNKS]
+        bq_rows = held.tile([P, P], F32, name="bq_rows")
+        nc.vector.memset(bq_rows[:], 0.0)
+        nc.sync.dma_start(bq_rows[0:HEADS, :], bq.rearrange("(h p) o -> h (p o)", p=P))
+        nc.sync.dma_start(wq_sb[0][:], wq_blocks[:, :, 0:P])
+        nc.sync.dma_start(x_f32[0][:], x_blocks[:, 0, :])
+        for chunk, (first, end) in zip(x_chunks, CHUNKS):
+            nc.sync.dma_start(chunk[:], x_blocks[:, first:end, :])
+
         offsets = held.tile([P, N // 16], U16, name="offsets")
         nc.sync.dma_start(offsets[:], offs)
+        for h in range(1, HEADS):
+            nc.sync.dma_start(wq_sb[h][:], wq_blocks[:, :, h * P:(h + 1) * P])
+            nc.sync.dma_start(x_f32[h][:], x_blocks[:, h, :])
 
         def piece_offsets(piece):
             return offsets[:, piece * PIECE // 16:(piece + 1) * PIECE // 16]
 
         ident = held.tile([P, P], F32, name="ident")
         make_identity(nc, ident[:])
-        bq_rows = held.tile([P, P], F32, name="bq_rows")
-        nc.vector.memset(bq_rows[:], 0.0)
-        nc.sync.dma_start(bq_rows[0:HEADS, :], bq.rearrange("(h p) o -> h (p o)", p=P))
         bq_ps = psum_once.tile([P, P], F32, name="bq_ps")
         nc.tensor.transpose(bq_ps[:], bq_rows[:], ident[:])
         bias = held.tile([P, HEADS], F32, name="bias")
         nc.vector.tensor_copy(bias[:], bq_ps[:, 0:HEADS])
+
 
         one_col = [held.tile([P, 2 * P], BF16, name=f"one_col_{odd}") for odd in range(2)]
         for odd in range(2):
@@ -61,16 +76,11 @@ def tile_multiheaddotproduct_kernel(tc, x, wq, bq, offs, out):
             first_col = P - row % 2 - row
             return one_col[row % 2][:, first_col:first_col + P]
 
-        x_f32 = [held.tile([P, S], F32, name=f"x_f32_{h}") for h in range(HEADS)]
-        x_bf = [held.tile([P, S], BF16, name=f"x_bf_{h}") for h in range(HEADS)]
-        wq_blocks = wq.rearrange("(ub p) c -> p ub c", p=P)
-        wq_sb = [held.tile([P, HEADS, P], BF16, name=f"wq_{h}") for h in range(HEADS)]
-        nc.sync.dma_start(wq_sb[0][:], wq_blocks[:, :, 0:P])
-        for h in range(HEADS):
-            nc.sync.dma_start(x_f32[h][:], x[h * P:(h + 1) * P, :])
-            nc.vector.tensor_copy(x_bf[h][:], x_f32[h][:])
-        for h in range(1, HEADS):
-            nc.sync.dma_start(wq_sb[h][:], wq_blocks[:, :, h * P:(h + 1) * P])
+        x_bf = [held.tile([P, S], BF16, name=f"x_bf_{ub}") for ub in range(HEADS)]
+        nc.vector.tensor_copy(x_bf[0][:], x_f32[0][:])
+        for chunk, (first, end) in zip(x_chunks, CHUNKS):
+            for ub in range(first, end):
+                nc.vector.tensor_copy(x_bf[ub][:], chunk[:, ub - first, :])
 
         park_rows = HEADS * N // S
         park = out[C - park_rows:C, :]

@@ -156,29 +156,30 @@ def tile_multiheaddotproduct_kernel(tc, x, wq, bq, offs, out):
                 nc.sync.dma_start(attn_all[h][:], head_park.partition_broadcast(P))
 
         for h in range(HEADS):
-            on_tensor = h not in (2 * GROUP - 1, HEADS - 1)
+            on_tensor = h < HEADS - 2
+            out_rows = out[h * P:(h + 1) * P, :]
             weighted = out_pool.tile([P, N], F32, name="weighted")
+            o_sb = out_pool.tile([P, S], F32, name="o_sb")
             if on_tensor:
-                planes = out_pool.tile([P, A, S], F32, name="planes")
+                planes = out_pool.tile([P, A // 2, S, 2], F32, name="planes")
             for piece in range(PIECES):
                 weighted_piece = weighted[:, piece * PIECE:(piece + 1) * PIECE]
                 nc.vector.tensor_tensor(weighted_piece, x_f32[h][:].indirect(piece_offsets(piece)),
                                         attn_all[h][:, piece * PIECE:(piece + 1) * PIECE], ALU.mult)
+                nodes = slice(piece * PIECE_NODES, (piece + 1) * PIECE_NODES)
+                by_node = weighted_piece.rearrange("p (i a) -> p i a", a=A)
                 if on_tensor:
-                    nc.scalar.copy(planes[:, :, piece * PIECE_NODES:(piece + 1) * PIECE_NODES]
-                                   .rearrange("p a i -> p i a"),
-                                   weighted_piece.rearrange("p (i a) -> p i a", a=A))
-            o_sb = out_pool.tile([P, S], F32, name="o_sb")
+                    nc.scalar.copy(planes[:, :, nodes, :],
+                                   weighted_piece.rearrange("p (i g b) -> p g i b", g=A // 2, b=2))
+                else:
+                    nc.vector.tensor_reduce(o_sb[:, nodes], by_node, axis=X_AXIS, op=ALU.add)
+                    nc.sync.dma_start(out_rows[:, nodes], o_sb[:, nodes])
             if on_tensor:
                 o_ps = psum.tile([P, S], F32, name="o_ps")
                 for half in range(2):
                     for a in range(A):
                         nc.tensor.matmul(o_ps[:, half * S // 2:(half + 1) * S // 2], lhsT=ident[:],
-                                         rhs=planes[:, a, half * S // 2:(half + 1) * S // 2],
+                                         rhs=planes[:, a // 2, half * S // 2:(half + 1) * S // 2, a % 2],
                                          start=(a == 0), stop=(a == A - 1))
                 nc.scalar.copy(o_sb[:], o_ps[:])
-                nc.scalar.dma_start(out[h * P:(h + 1) * P, :], o_sb[:])
-            else:
-                nc.vector.tensor_reduce(o_sb[:], weighted[:].rearrange("p (i a) -> p i a", a=A),
-                                        axis=X_AXIS, op=ALU.add)
-                nc.sync.dma_start(out[h * P:(h + 1) * P, :], o_sb[:])
+                nc.scalar.dma_start(out_rows, o_sb[:])

@@ -19,7 +19,7 @@ STRIP = 64
 STRIP_NODES = STRIP // A
 ROWS_A_HEAD = N // STRIP
 GROUP = 3
-CHUNKS = ((1, 3), (3, 5), (5, 7), (7, 8))
+CHUNKS = ((0, 3), (3, 5), (5, 7), (7, 8))
 STORE_ROWS = 64
 SCALE = 1.0 / math.sqrt(P)
 
@@ -37,24 +37,25 @@ def tile_multiheaddotproduct_kernel(tc, x, wq, bq, offs, out):
         psum_once = ctx.enter_context(tc.psum_pool(name="psum_once", bufs=1))
         psum = ctx.enter_context(tc.psum_pool(name="psum", bufs=2))
 
-        x_blocks = x.rearrange("(ub p) s -> p ub s", p=P)
-        wq_blocks = wq.rearrange("(ub p) c -> p ub c", p=P)
+        x_by_sum = x.rearrange("(p ub) s -> p ub s", p=P)
+        wq_by_sum = wq.rearrange("(p ub) c -> p ub c", p=P)
+        x_by_head = x.rearrange("(h p) s -> p h s", p=P)
         wq_sb = [held.tile([P, HEADS, P], BF16, name=f"wq_{h}") for h in range(HEADS)]
         x_f32 = [held.tile([P, S], F32, name=f"x_f32_{h}") for h in range(HEADS)]
         x_chunks = [held.tile([P, end - first, S], F32, name=f"x_chunk_{first}") for first, end in CHUNKS]
         bq_rows = held.tile([P, P], F32, name="bq_rows")
         nc.vector.memset(bq_rows[:], 0.0)
         nc.sync.dma_start(bq_rows[0:HEADS, :], bq.rearrange("(h p) o -> h (p o)", p=P))
-        nc.sync.dma_start(wq_sb[0][:], wq_blocks[:, :, 0:P])
-        nc.sync.dma_start(x_f32[0][:], x_blocks[:, 0, :])
+        nc.sync.dma_start(wq_sb[0][:], wq_by_sum[:, :, 0:P])
         for chunk, (first, end) in zip(x_chunks, CHUNKS):
-            nc.sync.dma_start(chunk[:], x_blocks[:, first:end, :])
+            nc.sync.dma_start(chunk[:], x_by_sum[:, first:end, :])
+        nc.sync.dma_start(x_f32[0][:], x_by_head[:, 0, :])
 
         offsets = held.tile([P, N // 16], U16, name="offsets")
         nc.sync.dma_start(offsets[:], offs)
         for h in range(1, HEADS):
-            nc.sync.dma_start(wq_sb[h][:], wq_blocks[:, :, h * P:(h + 1) * P])
-            nc.sync.dma_start(x_f32[h][:], x_blocks[:, h, :])
+            nc.sync.dma_start(wq_sb[h][:], wq_by_sum[:, :, h * P:(h + 1) * P])
+            nc.sync.dma_start(x_f32[h][:], x_by_head[:, h, :])
 
         def piece_offsets(piece):
             return offsets[:, piece * PIECE // 16:(piece + 1) * PIECE // 16]
@@ -77,7 +78,6 @@ def tile_multiheaddotproduct_kernel(tc, x, wq, bq, offs, out):
             return one_col[row % 2][:, first_col:first_col + P]
 
         x_bf = [held.tile([P, S], BF16, name=f"x_bf_{ub}") for ub in range(HEADS)]
-        nc.vector.tensor_copy(x_bf[0][:], x_f32[0][:])
         for chunk, (first, end) in zip(x_chunks, CHUNKS):
             for ub in range(first, end):
                 nc.vector.tensor_copy(x_bf[ub][:], chunk[:, ub - first, :])
@@ -156,7 +156,7 @@ def tile_multiheaddotproduct_kernel(tc, x, wq, bq, offs, out):
                 nc.sync.dma_start(attn_all[h][:], head_park.partition_broadcast(P))
 
         for h in range(HEADS):
-            on_tensor = h < HEADS - 2
+            on_tensor = h < HEADS - 1
             out_rows = out[h * P:(h + 1) * P, :]
             weighted = out_pool.tile([P, N], F32, name="weighted")
             o_sb = out_pool.tile([P, S], F32, name="o_sb")

@@ -85,7 +85,7 @@ def tile_multiheaddotproduct_kernel(tc, x, wq, bq, offs, out):
         park_rows = HEADS * N // S
         park = out[C - park_rows:C, :]
         park_by_strip = park.rearrange("r (s t) -> (r s) t", t=STRIP)
-        attn_all = [held.tile([P, N], F32, name=f"attn_all_{h}") for h in range(HEADS)]
+        attn_all = held.tile([P, HEADS * N], F32, name="attn_all")
 
         def project(h):
             q_ps = psum.tile([P, S], F32, name="q_ps")
@@ -151,9 +151,9 @@ def tile_multiheaddotproduct_kernel(tc, x, wq, bq, offs, out):
 
             store_end = min(first_row + STORE_ROWS, P)
             nc.sync.dma_start(park_by_strip[first_row:store_end, :], attn[first_row:store_end, :])
-            for h in range(first_head, end_head):
-                head_park = park[h * N // S:(h + 1) * N // S, :].rearrange("r c -> (r c)")
-                nc.sync.dma_start(attn_all[h][:], head_park.partition_broadcast(P))
+            for first, end in ((first_head, first_head + 1), (first_head + 1, end_head)):
+                heads_park = park[first * N // S:end * N // S, :].rearrange("r c -> (r c)")
+                nc.sync.dma_start(attn_all[:, first * N:end * N], heads_park.partition_broadcast(P))
 
         for h in range(HEADS):
             on_tensor = h < HEADS - 1
@@ -165,7 +165,8 @@ def tile_multiheaddotproduct_kernel(tc, x, wq, bq, offs, out):
             for piece in range(PIECES):
                 weighted_piece = weighted[:, piece * PIECE:(piece + 1) * PIECE]
                 nc.vector.tensor_tensor(weighted_piece, x_f32[h][:].indirect(piece_offsets(piece)),
-                                        attn_all[h][:, piece * PIECE:(piece + 1) * PIECE], ALU.mult)
+                                        attn_all[:, h * N + piece * PIECE:h * N + (piece + 1) * PIECE],
+                                        ALU.mult)
                 nodes = slice(piece * PIECE_NODES, (piece + 1) * PIECE_NODES)
                 by_node = weighted_piece.rearrange("p (i a) -> p i a", a=A)
                 if on_tensor:

@@ -151,7 +151,8 @@ def tile_multiheaddotproduct_kernel(tc, x, wq, bq, offs, out):
 
             store_end = min(first_row + STORE_ROWS, P)
             nc.sync.dma_start(park_by_strip[first_row:store_end, :], attn[first_row:store_end, :])
-            for first, end in ((first_head, first_head + 1), (first_head + 1, end_head)):
+            bounds = (0, 1, end_head) if first_head == 0 else (first_head, end_head)
+            for first, end in zip(bounds[:-1], bounds[1:]):
                 heads_park = park[first * N // S:end * N // S, :].rearrange("r c -> (r c)")
                 nc.sync.dma_start(attn_all[:, first * N:end * N], heads_park.partition_broadcast(P))
 

from contextlib import ExitStack
import math

import concourse.mybir as mybir
from concourse.masks import make_identity

F32, BF16, U16 = mybir.dt.float32, mybir.dt.bfloat16, mybir.dt.uint16
ALU = mybir.AluOpType
ACT = mybir.ActivationFunctionType
X_AXIS = mybir.AxisListType.X

P = 128
C, S, N, A = 1024, 256, 1024, 4
HEADS = C // P
PIECE = 256
PIECES = N // PIECE
PIECE_NODES = PIECE // A
STRIP = 64
STRIP_NODES = STRIP // A
ROWS_A_HEAD = N // STRIP
GROUP = 3
CHUNKS = ((0, 3), (3, 5), (5, 7), (7, 8))
STORE_ROWS = 64
SCALE = 1.0 / math.sqrt(P)

FLOPS = 2 * C * C * S + 4 * C * N


def tile_multiheaddotproduct_kernel(tc, x, wq, bq, offs, out):
    nc = tc.nc
    with ExitStack() as ctx:
        held = ctx.enter_context(tc.tile_pool(name="held", bufs=1))
        q_pool = ctx.enter_context(tc.tile_pool(name="q_pool", bufs=3))
        prod_pool = ctx.enter_context(tc.tile_pool(name="prod_pool", bufs=4))
        soft_pool = ctx.enter_context(tc.tile_pool(name="soft_pool", bufs=2))
        out_pool = ctx.enter_context(tc.tile_pool(name="out_pool", bufs=4))
        psum_once = ctx.enter_context(tc.psum_pool(name="psum_once", bufs=1))
        psum = ctx.enter_context(tc.psum_pool(name="psum", bufs=2))

        x_by_sum = x.rearrange("(p ub) s -> p ub s", p=P)
        wq_by_sum = wq.rearrange("(p ub) c -> p ub c", p=P)
        x_by_head = x.rearrange("(h p) s -> p h s", p=P)
        wq_sb = [held.tile([P, HEADS, P], BF16, name=f"wq_{h}") for h in range(HEADS)]
        x_f32 = [held.tile([P, S], F32, name=f"x_f32_{h}") for h in range(HEADS)]
        x_chunks = [held.tile([P, end - first, S], F32, name=f"x_chunk_{first}") for first, end in CHUNKS]
        bq_rows = held.tile([P, P], F32, name="bq_rows")
        nc.vector.memset(bq_rows[:], 0.0)
        nc.sync.dma_start(bq_rows[0:HEADS, :], bq.rearrange("(h p) o -> h (p o)", p=P))
        nc.sync.dma_start(wq_sb[0][:], wq_by_sum[:, :, 0:P])
        for chunk, (first, end) in zip(x_chunks, CHUNKS):
            nc.sync.dma_start(chunk[:], x_by_sum[:, first:end, :])
        nc.sync.dma_start(x_f32[0][:], x_by_head[:, 0, :])

        offsets = held.tile([P, N // 16], U16, name="offsets")
        nc.sync.dma_start(offsets[:], offs)
        for h in range(1, HEADS):
            nc.sync.dma_start(wq_sb[h][:], wq_by_sum[:, :, h * P:(h + 1) * P])
            nc.sync.dma_start(x_f32[h][:], x_by_head[:, h, :])

        def piece_offsets(piece):
            return offsets[:, piece * PIECE // 16:(piece + 1) * PIECE // 16]

        ident = held.tile([P, P], F32, name="ident")
        make_identity(nc, ident[:])
        bq_ps = psum_once.tile([P, P], F32, name="bq_ps")
        nc.tensor.transpose(bq_ps[:], bq_rows[:], ident[:])
        bias = held.tile([P, HEADS], F32, name="bias")
        nc.vector.tensor_copy(bias[:], bq_ps[:, 0:HEADS])


        one_col = [held.tile([P, 2 * P], BF16, name=f"one_col_{odd}") for odd in range(2)]
        for odd in range(2):
            nc.vector.memset(one_col[odd][:], 0.0)
            nc.vector.memset(one_col[odd][:, P - odd:P - odd + 1], 1.0)

        def sum_into_row(row):
            first_col = P - row % 2 - row
            return one_col[row % 2][:, first_col:first_col + P]

        x_bf = [held.tile([P, S], BF16, name=f"x_bf_{ub}") for ub in range(HEADS)]
        for chunk, (first, end) in zip(x_chunks, CHUNKS):
            for ub in range(first, end):
                nc.vector.tensor_copy(x_bf[ub][:], chunk[:, ub - first, :])

        park_rows = HEADS * N // S
        park = out[C - park_rows:C, :]
        park_by_strip = park.rearrange("r (s t) -> (r s) t", t=STRIP)
        attn_all = held.tile([P, HEADS * N], F32, name="attn_all")

        def project(h):
            q_ps = psum.tile([P, S], F32, name="q_ps")
            for ub in range(HEADS):
                nc.tensor.matmul(q_ps[:], lhsT=wq_sb[h][:, ub, :], rhs=x_bf[ub][:],
                                 start=(ub == 0), stop=(ub == HEADS - 1))
            q_rep = q_pool.tile([P, N], F32, name="q_rep")
            cuts = PIECES if h == 0 else 1
            for cut in range(cuts):
                nc.scalar.activation(
                    q_rep[:, cut * N // cuts:(cut + 1) * N // cuts].rearrange("p (i a) -> p i a", a=A),
                    q_ps[:, cut * S // cuts:(cut + 1) * S // cuts]
                    .unsqueeze(2).to_broadcast([P, S // cuts, A]),
                    ACT.Identity, bias=bias[:, h:h + 1])
            return q_rep

        q_next = project(0)
        for first_head in range(0, HEADS, GROUP):
            end_head = min(first_head + GROUP, HEADS)
            first_row, end_row = first_head * ROWS_A_HEAD, end_head * ROWS_A_HEAD
            sims = psum.tile([P, STRIP], F32, name="sims")
            for h in range(first_head, end_head):
                q_rep = q_next
                if h + 1 < HEADS:
                    q_next = project(h + 1)

                for pair in range(PIECES // 2):
                    prod = prod_pool.tile([P, 2 * PIECE], F32, name="prod")
                    prod_bf = prod_pool.tile([P, 2 * PIECE], BF16, name="prod_bf")
                    last_of_group = h == end_head - 1 and pair == PIECES // 2 - 1
                    for piece in (2 * pair, 2 * pair + 1):
                        cols = slice((piece % 2) * PIECE, (piece % 2 + 1) * PIECE)
                        nc.vector.tensor_tensor(prod[:, cols], x_f32[h][:].indirect(piece_offsets(piece)),
                                                q_rep[:, piece * PIECE:(piece + 1) * PIECE], ALU.mult)
                        if last_of_group:
                            nc.scalar.copy(prod_bf[:, cols], prod[:, cols])
                    if not last_of_group:
                        nc.scalar.copy(prod_bf[:], prod[:])
                    for s in range(2 * PIECE // STRIP):
                        row = h * ROWS_A_HEAD + pair * (2 * PIECE // STRIP) + s
                        nc.tensor.matmul(sims[:], lhsT=sum_into_row(row),
                                         rhs=prod_bf[:, s * STRIP:(s + 1) * STRIP],
                                         start=(row == first_row), stop=(row == end_row - 1))

            sims_by_node = sims[:].rearrange("p (i a) -> p i a", a=A)
            top = soft_pool.tile([P, STRIP_NODES], F32, name="top")
            nc.vector.tensor_reduce(top[:], sims_by_node, axis=X_AXIS, op=ALU.max)
            shifted = soft_pool.tile([P, STRIP], F32, name="shifted")
            nc.vector.tensor_tensor(shifted[:].rearrange("p (i a) -> p i a", a=A), sims_by_node,
                                    top[:].unsqueeze(2).to_broadcast([P, STRIP_NODES, A]),
                                    ALU.subtract)
            e = soft_pool.tile([P, STRIP], F32, name="e")
            nc.scalar.activation(e[:], shifted[:], ACT.Exp, scale=SCALE)
            e_by_node = e[:].rearrange("p (i a) -> p i a", a=A)
            den = soft_pool.tile([P, STRIP_NODES], F32, name="den")
            nc.vector.tensor_reduce(den[:], e_by_node, axis=X_AXIS, op=ALU.add)
            rden = soft_pool.tile([P, STRIP_NODES], F32, name="rden")
            nc.vector.reciprocal(rden[:], den[:])
            attn = soft_pool.tile([P, STRIP], F32, name="attn")
            nc.vector.tensor_tensor(attn[:].rearrange("p (i a) -> p i a", a=A), e_by_node,
                                    rden[:].unsqueeze(2).to_broadcast([P, STRIP_NODES, A]),
                                    ALU.mult)

            store_end = min(first_row + STORE_ROWS, P)
            nc.sync.dma_start(park_by_strip[first_row:store_end, :], attn[first_row:store_end, :])
            bounds = (0, 1, end_head) if first_head == 0 else (first_head, end_head)
            for first, end in zip(bounds[:-1], bounds[1:]):
                heads_park = park[first * N // S:end * N // S, :].rearrange("r c -> (r c)")
                nc.sync.dma_start(attn_all[:, first * N:end * N], heads_park.partition_broadcast(P))

        for h in range(HEADS):
            on_tensor = h < HEADS - 1
            out_rows = out[h * P:(h + 1) * P, :]
            weighted = out_pool.tile([P, N], F32, name="weighted")
            o_sb = out_pool.tile([P, S], F32, name="o_sb")
            if on_tensor:
                planes = out_pool.tile([P, A // 2, S, 2], F32, name="planes")
            for piece in range(PIECES):
                weighted_piece = weighted[:, piece * PIECE:(piece + 1) * PIECE]
                nc.vector.tensor_tensor(weighted_piece, x_f32[h][:].indirect(piece_offsets(piece)),
                                        attn_all[:, h * N + piece * PIECE:h * N + (piece + 1) * PIECE],
                                        ALU.mult)
                nodes = slice(piece * PIECE_NODES, (piece + 1) * PIECE_NODES)
                by_node = weighted_piece.rearrange("p (i a) -> p i a", a=A)
                if on_tensor:
                    nc.scalar.copy(planes[:, :, nodes, :],
                                   weighted_piece.rearrange("p (i g b) -> p g i b", g=A // 2, b=2))
                else:
                    nc.vector.tensor_reduce(o_sb[:, nodes], by_node, axis=X_AXIS, op=ALU.add)
                    nc.sync.dma_start(out_rows[:, nodes], o_sb[:, nodes])
            if on_tensor:
                o_ps = psum.tile([P, S], F32, name="o_ps")
                for half in range(2):
                    for a in range(A):
                        nc.tensor.matmul(o_ps[:, half * S // 2:(half + 1) * S // 2], lhsT=ident[:],
                                         rhs=planes[:, a // 2, half * S // 2:(half + 1) * S // 2, a % 2],
                                         start=(a == 0), stop=(a == A - 1))
                nc.scalar.copy(o_sb[:], o_ps[:])
                nc.scalar.dma_start(out_rows, o_sb[:])
